import numpy as np
import ml_dtypes


def mxq(x, axis, fmt="e4m3"):
    dtype, down = {"e4m3": (ml_dtypes.float8_e4m3fn, 7), "e5m2": (ml_dtypes.float8_e5m2, 14)}[fmt]
    v = np.moveaxis(np.asarray(x, np.float32).astype(ml_dtypes.bfloat16).astype(np.float64), axis, -1)
    blocks = v.reshape(v.shape[:-1] + (-1, 32))
    amax = np.abs(blocks).max(-1, keepdims=True)
    byte = np.maximum(np.where(amax > 0, np.frexp(amax)[1] - 1 + 127, 0) - down, 1)
    scale = np.exp2(byte - 127.0)
    codes = (blocks / scale).astype(np.float32).astype(dtype).astype(np.float64)
    return np.moveaxis((codes * scale).reshape(v.shape), -1, axis)


WIDE = False


def mx_kscale(k):
    if not WIDE:
        return np.ones(k)
    levels = np.array([10, -10, 5, -5, 0])
    a = np.random.permutation(np.resize(levels, k // 512 * 4)).reshape(k // 512, 4)
    idx = np.arange(k)
    return np.exp2(a[idx // 512, idx % 128 // 32])


BF16 = ml_dtypes.bfloat16


def bf(x):
    return np.asarray(x, np.float32).astype(BF16)


def f64(x):
    return np.asarray(x).astype(np.float64)


B, I, H = 4096, 512, 512
G = 2 * H
EPS = 1e-5


def ln(v):
    mu = v.mean(-1, keepdims=True)
    var = np.square(v - mu).mean(-1, keepdims=True)
    return (v - mu) / np.sqrt(var + EPS)


def sigmoid(v):
    return 1.0 / (1.0 + np.exp(-v))


def setup_inputs():
    s, t = mx_kscale(I), mx_kscale(H)
    return {"x": bf(np.random.standard_normal((B, I)) * s),
            "h": bf(np.random.standard_normal((B, H)) * t),
            "W_irz": bf(np.random.standard_normal((G, I)) / np.sqrt(I) / s),
            "b_irz": bf(np.random.standard_normal(G) * 0.5),
            "W_hrz": bf(np.random.standard_normal((G, H)) / np.sqrt(H) / t),
            "b_hrz": bf(np.random.standard_normal(G) * 0.5)}


def reference(x, h, W_irz, b_irz, W_hrz, b_hrz):
    i_rz = ln((mxq(f64(x), 1, "e4m3") @ mxq(f64(W_irz), 1, "e4m3").T) + f64(b_irz))
    h_rz = ln((mxq(f64(h), 1, "e4m3") @ mxq(f64(W_hrz), 1, "e4m3").T) + f64(b_hrz))
    return sigmoid(i_rz + h_rz)

@@ -1,0 +1,229 @@
+from contextlib import ExitStack
+
+import concourse.bass as bass
+import concourse.mybir as mybir
+import concourse.tile as tile
+from concourse.masks import make_identity
+
+F32 = mybir.dt.float32
+BF16 = mybir.dt.bfloat16
+U32 = mybir.dt.uint32
+U8 = mybir.dt.uint8
+FP8X4 = mybir.dt.float8_e4m3fn_x4
+ALU = mybir.AluOpType
+ACT = mybir.ActivationFunctionType
+
+P = 128
+B = 4096
+K = 512
+N = 1024
+NT = B // P
+T = 2
+NG = NT // T
+EPS = 1e-5
+FLOPS = 2 * 2 * B * K * N
+
+CHUNKS = [(0, 2), (2, 6), (8, 8), (16, 8), (24, 8)]
+
+
+def tile_layernormgrucell_pa_t_kernel(tc, x, h, W_irz, b_irz, W_hrz, b_hrz, out):
+    nc = tc.nc
+    with ExitStack() as ctx:
+        const = ctx.enter_context(tc.tile_pool(name="const", bufs=1))
+        wgp = ctx.enter_context(tc.tile_pool(name="wgp", bufs=2))
+        xgp = ctx.enter_context(tc.tile_pool(name="xgp", bufs=2))
+        xcp = ctx.enter_context(tc.tile_pool(name="xcp", bufs=3))
+        abp = ctx.enter_context(tc.tile_pool(name="abp", bufs=3))
+        op = ctx.enter_context(tc.tile_pool(name="op", bufs=3))
+        jp = ctx.enter_context(tc.tile_pool(name="jp", bufs=2))
+        stp = ctx.enter_context(tc.tile_pool(name="stp", bufs=4))
+        tpp = ctx.enter_context(tc.psum_pool(name="tpp", bufs=2))
+        mmp = ctx.enter_context(tc.psum_pool(name="mmp", bufs=6))
+
+        ident = const.tile([P, P], F32, name="ident")
+        make_identity(nc, ident[:])
+        ones = const.tile([P, P], BF16, name="ones")
+        nc.vector.memset(ones[:], 1.0)
+        mhalf = const.tile([P, 2 * T], F32, name="mhalf")
+        nc.vector.memset(mhalf[:], -0.5)
+        warm = const.tile([P, 1], F32, name="warm")
+        nc.scalar.activation(out=warm[:], in_=mhalf[:, 0:1], func=ACT.Sigmoid)
+        brow = const.tile([P, 2 * N], BF16, name="brow")
+        nc.vector.memset(brow[:], 0.0)
+        nc.scalar.dma_start(out=brow[0:1, 0:N], in_=b_irz.rearrange("(o n) -> o n", o=1))
+        nc.scalar.dma_start(out=brow[0:1, N : 2 * N], in_=b_hrz.rearrange("(o n) -> o n", o=1))
+
+        acts = (x, h)
+        wts = (W_irz, W_hrz)
+        xch = [[None] * len(CHUNKS), [None] * len(CHUNKS)]
+        wraw = [[None, None], [None, None]]
+
+        def load_act(o, ci):
+            t0, nt = CHUNKS[ci]
+            t_ = const.tile([P, nt * K], BF16, name="act%d_%d" % (o, ci))
+            nc.sync.dma_start(
+                out=t_[:].rearrange("p (t k) -> p t k", k=K),
+                in_=acts[o].rearrange("(p t) k -> p t k", t=NT)[:, t0 : t0 + nt, :],
+            )
+            xch[o][ci] = t_
+
+        def load_w(o, hf):
+            t_ = const.tile([P, 4 * K], BF16, name="wraw%d_%d" % (o, hf))
+            nc.sync.dma_start(
+                out=t_[:].rearrange("p (j k) -> p j k", k=K),
+                in_=wts[o][hf * 512 : (hf + 1) * 512, :].rearrange("(j p) k -> p j k", p=P),
+            )
+            wraw[o][hf] = t_
+
+        load_w(0, 0)
+        load_act(0, 0)
+        load_w(0, 1)
+        load_act(1, 0)
+        load_w(1, 0)
+        load_w(1, 1)
+        for ci in range(1, len(CHUNKS)):
+            load_act(0, ci)
+            load_act(1, ci)
+
+        bias = const.tile([P, 2 * N], F32, name="bias")
+        for q in range(4):
+            ps = mmp.tile([P, 512], F32, tag="mm", name="ps")
+            nc.tensor.matmul(out=ps[:], lhsT=ones[:], rhs=brow[:, q * 512 : (q + 1) * 512], start=True, stop=True)
+            nc.vector.tensor_copy(out=bias[:, q * 512 : (q + 1) * 512], in_=ps[:])
+
+        wc = [const.tile([P, N], U32, name="wc%d" % o, align_bytes=64) for o in range(2)]
+        wsc = [const.tile([P, N], U8, name="wsc%d" % o, align_bytes=64) for o in range(2)]
+
+        def prep_w(o, hf):
+            raw_w = wraw[o][hf][:].bitcast(F32)
+            wg = wgp.tile([P, 2048], BF16, tag="wg", name="wg", align_bytes=64)
+            wg_w = wg[:].bitcast(F32)
+            for pr in range(2):
+                tp = tpp.tile([P, 4, P], F32, tag="tp", name="tp")
+                for jj in range(2):
+                    for u in range(2):
+                        c0 = (2 * pr + jj) * 256 + u * 128
+                        nc.tensor.transpose(tp[:, 2 * jj + u, :], raw_w[:, c0 : c0 + 128], ident[:])
+                dst = wg_w[:, pr * 512 : (pr + 1) * 512].rearrange("p (a r u) -> p a r u", a=2, u=2)
+                src = tp[:].rearrange("p (a u) r -> p a r u", u=2)
+                if pr == 0:
+                    nc.vector.tensor_copy(out=dst, in_=src)
+                else:
+                    nc.scalar.copy(out=dst, in_=src)
+            cols = slice(hf * 512, (hf + 1) * 512)
+            nc.vector.quantize_mx(out=wc[o][:, cols].bitcast(FP8X4), scales=wsc[o][:, cols], in_=wg[:])
+
+        def act_words(o, t):
+            for ci in range(len(CHUNKS)):
+                t0, nt = CHUNKS[ci]
+                if t0 <= t < t0 + nt:
+                    return xch[o][ci][:].bitcast(F32)[:, (t - t0) * 256 : (t - t0 + 1) * 256]
+            raise ValueError("no chunk")
+
+        def stage_a(g):
+            xg = xgp.tile([P, T * 1024], BF16, tag="xg", name="xg", align_bytes=64)
+            xg_w = xg[:].bitcast(F32)
+            for tt in range(T):
+                tp = tpp.tile([P, 4, P], F32, tag="tp", name="tp")
+                for o in range(2):
+                    w_ = act_words(o, g * T + tt)
+                    for u in range(2):
+                        nc.tensor.transpose(tp[:, 2 * o + u, :], w_[:, u * 128 : (u + 1) * 128], ident[:])
+                dst = xg_w[:, tt * 512 : (tt + 1) * 512].rearrange("p (a r u) -> p a r u", a=2, u=2)
+                nc.scalar.copy(out=dst, in_=tp[:].rearrange("p (a u) r -> p a r u", u=2))
+            xc = xcp.tile([P, T * 256], U32, tag="xc", name="xc", align_bytes=64)
+            xs = xcp.tile([P, T * 256], U8, tag="xs", name="xs", align_bytes=64)
+            nc.vector.quantize_mx(out=xc[:].bitcast(FP8X4), scales=xs[:], in_=xg[:])
+            return xc, xs
+
+        def stage_b(g, xc, xs):
+            ab = abp.tile([P, T, 2, N], F32, tag="ab", name="ab")
+            sv = stp.tile([P, 2, 2 * T], F32, tag="sv", name="sv")
+            for tt in range(T):
+                for o in range(2):
+                    i = tt * 2 + o
+                    for hf in range(2):
+                        cols = slice(hf * 512, (hf + 1) * 512)
+                        ps = mmp.tile([P, 512], F32, tag="mm", name="ps")
+                        nc.tensor.matmul_mx(
+                            out=ps[:],
+                            lhsT=xc[:, i * P : (i + 1) * P].bitcast(FP8X4),
+                            lhsT_scale=xs[:, i * P : (i + 1) * P],
+                            rhs=wc[o][:, cols].bitcast(FP8X4),
+                            rhs_scale=wsc[o][:, cols],
+                            start=True,
+                            stop=True,
+                        )
+                        nc.vector.scalar_tensor_tensor(
+                            out=ab[:, tt, o, cols],
+                            in0=ps[:],
+                            scalar=1.0,
+                            in1=bias[:, o * N + hf * 512 : o * N + (hf + 1) * 512],
+                            op0=ALU.mult,
+                            op1=ALU.add,
+                            accum_out=sv[:, hf, i : i + 1],
+                        )
+            sm = stp.tile([P, 2 * T], F32, tag="sm", name="sm")
+            nc.vector.tensor_tensor(out=sm[:], in0=sv[:, 0, :], in1=sv[:, 1, :], op=ALU.add)
+            negmu = stp.tile([P, 2 * T], F32, tag="negmu", name="negmu")
+            nc.vector.tensor_scalar(out=negmu[:], in0=sm[:], scalar1=-1.0 / N, scalar2=None, op0=ALU.mult)
+            ss = stp.tile([P, 2 * T], F32, tag="ss", name="ss")
+            for i in range(2 * T):
+                junk = jp.tile([P, N], BF16, tag="junk", name="junk")
+                nc.scalar.activation(
+                    out=junk[:],
+                    in_=ab[:, i // 2, i % 2, :],
+                    func=ACT.Square,
+                    bias=negmu[:, i : i + 1],
+                    scale=1.0,
+                    accum_out=ss[:, i : i + 1],
+                )
+            return ab, negmu, ss
+
+        def stage_c(g, ab, negmu, ss):
+            ve = stp.tile([P, 2 * T], F32, tag="ve", name="ve")
+            nc.gpsimd.tensor_scalar(out=ve[:], in0=ss[:], scalar1=1.0 / N, scalar2=EPS, op0=ALU.mult, op1=ALU.add)
+            rs = stp.tile([P, 2 * T], F32, tag="rs", name="rs")
+            nc.gpsimd.tensor_tensor(out=rs[:], in0=ve[:], in1=mhalf[:], op=ALU.pow)
+            ve_v = ve[:].rearrange("p (t o) -> p t o", o=2)
+            rs_v = rs[:].rearrange("p (t o) -> p t o", o=2)
+            sd = stp.tile([P, T], F32, tag="sd", name="sd")
+            nc.gpsimd.tensor_tensor(out=sd[:], in0=ve_v[:, :, 1], in1=rs_v[:, :, 1], op=ALU.mult)
+            rho = stp.tile([P, T], F32, tag="rho", name="rho")
+            nc.gpsimd.tensor_tensor(out=rho[:], in0=sd[:], in1=rs_v[:, :, 0], op=ALU.mult)
+            m = stp.tile([P, 2 * T], F32, tag="m", name="m")
+            nc.gpsimd.tensor_tensor(out=m[:], in0=negmu[:], in1=rs[:], op=ALU.mult)
+            m_v = m[:].rearrange("p (t o) -> p t o", o=2)
+            c = stp.tile([P, T], F32, tag="c", name="c")
+            nc.gpsimd.tensor_tensor(out=c[:], in0=m_v[:, :, 0], in1=m_v[:, :, 1], op=ALU.add)
+            ot = op.tile([P, T, N], F32, tag="ot", name="ot")
+            for tt in range(T):
+                nc.vector.scalar_tensor_tensor(
+                    out=ab[:, tt, 1, :],
+                    in0=ab[:, tt, 0, :],
+                    scalar=rho[:, tt : tt + 1],
+                    in1=ab[:, tt, 1, :],
+                    op0=ALU.mult,
+                    op1=ALU.add,
+                )
+                nc.scalar.activation(
+                    out=ot[:, tt, :],
+                    in_=ab[:, tt, 1, :],
+                    func=ACT.Sigmoid,
+                    bias=c[:, tt : tt + 1],
+                    scale=rs[:, 2 * tt + 1 : 2 * tt + 2],
+                )
+            nc.sync.dma_start(
+                out=out.rearrange("(p t) j -> p t j", t=NT)[:, g * T : (g + 1) * T, :],
+                in_=ot[:],
+            )
+
+        prep_w(0, 0)
+        q0 = stage_a(0)
+        prep_w(0, 1)
+        prep_w(1, 0)
+        prep_w(1, 1)
+        for g in range(NG):
+            xc, xs = q0 if g == 0 else stage_a(g)
+            ab, negmu, ss = stage_b(g, xc, xs)
+            stage_c(g, ab, negmu, ss)

@@ -1,8 +1,6 @@
 from contextlib import ExitStack
 
-import concourse.bass as bass
 import concourse.mybir as mybir
-import concourse.tile as tile
 from concourse.masks import make_identity
 
 F32 = mybir.dt.float32
@@ -18,12 +16,14 @@ B = 4096
 K = 512
 N = 1024
 NT = B // P
-T = 2
-NG = NT // T
 EPS = 1e-5
 FLOPS = 2 * 2 * B * K * N
-
 CHUNKS = [(0, 2), (2, 6), (8, 8), (16, 8), (24, 8)]
+
+EV_ON_VECTOR = 0
+LAG = 2
+GP5 = 0
+AB_BUFS = 5
 
 
 def tile_layernormgrucell_pa_t_kernel(tc, x, h, W_irz, b_irz, W_hrz, b_hrz, out):
@@ -31,27 +31,28 @@ def tile_layernormgrucell_pa_t_kernel(tc, x, h, W_irz, b_irz, W_hrz, b_hrz, out)
     with ExitStack() as ctx:
         const = ctx.enter_context(tc.tile_pool(name="const", bufs=1))
         wgp = ctx.enter_context(tc.tile_pool(name="wgp", bufs=2))
-        xgp = ctx.enter_context(tc.tile_pool(name="xgp", bufs=2))
-        xcp = ctx.enter_context(tc.tile_pool(name="xcp", bufs=3))
-        abp = ctx.enter_context(tc.tile_pool(name="abp", bufs=3))
-        op = ctx.enter_context(tc.tile_pool(name="op", bufs=3))
+        xgp = ctx.enter_context(tc.tile_pool(name="xgp", bufs=3))
+        xcp = ctx.enter_context(tc.tile_pool(name="xcp", bufs=2))
+        abp = ctx.enter_context(tc.tile_pool(name="abp", bufs=AB_BUFS))
+        op = ctx.enter_context(tc.tile_pool(name="op", bufs=4))
         jp = ctx.enter_context(tc.tile_pool(name="jp", bufs=2))
-        stp = ctx.enter_context(tc.tile_pool(name="stp", bufs=4))
-        tpp = ctx.enter_context(tc.psum_pool(name="tpp", bufs=2))
-        mmp = ctx.enter_context(tc.psum_pool(name="mmp", bufs=6))
+        stp = ctx.enter_context(tc.tile_pool(name="stp", bufs=AB_BUFS + 2))
+        psp = ctx.enter_context(tc.psum_pool(name="psp", bufs=8))
+        ctx.enter_context(tc.manual_schedule())
+
+        def bank():
+            return psp.tile([P, 512], F32, tag="bank", name="bank")
 
         ident = const.tile([P, P], F32, name="ident")
         make_identity(nc, ident[:])
+        brow = const.tile([P, 2 * N], BF16, name="brow")
+        nc.vector.memset(brow[:].bitcast(mybir.dt.int32), 0)
         ones = const.tile([P, P], BF16, name="ones")
         nc.vector.memset(ones[:], 1.0)
-        mhalf = const.tile([P, 2 * T], F32, name="mhalf")
+        mhalf = const.tile([P, 2], F32, name="mhalf")
         nc.vector.memset(mhalf[:], -0.5)
         warm = const.tile([P, 1], F32, name="warm")
         nc.scalar.activation(out=warm[:], in_=mhalf[:, 0:1], func=ACT.Sigmoid)
-        brow = const.tile([P, 2 * N], BF16, name="brow")
-        nc.vector.memset(brow[:], 0.0)
-        nc.scalar.dma_start(out=brow[0:1, 0:N], in_=b_irz.rearrange("(o n) -> o n", o=1))
-        nc.scalar.dma_start(out=brow[0:1, N : 2 * N], in_=b_hrz.rearrange("(o n) -> o n", o=1))
 
         acts = (x, h)
         wts = (W_irz, W_hrz)
@@ -77,8 +78,10 @@ def tile_layernormgrucell_pa_t_kernel(tc, x, h, W_irz, b_irz, W_hrz, b_hrz, out)
 
         load_w(0, 0)
         load_act(0, 0)
-        load_w(0, 1)
         load_act(1, 0)
+        nc.sync.dma_start(out=brow[0:1, 0:N], in_=b_irz.rearrange("(o n) -> o n", o=1))
+        nc.sync.dma_start(out=brow[0:1, N : 2 * N], in_=b_hrz.rearrange("(o n) -> o n", o=1))
+        load_w(0, 1)
         load_w(1, 0)
         load_w(1, 1)
         for ci in range(1, len(CHUNKS)):
@@ -86,32 +89,40 @@ def tile_layernormgrucell_pa_t_kernel(tc, x, h, W_irz, b_irz, W_hrz, b_hrz, out)
             load_act(1, ci)
 
         bias = const.tile([P, 2 * N], F32, name="bias")
-        for q in range(4):
-            ps = mmp.tile([P, 512], F32, tag="mm", name="ps")
-            nc.tensor.matmul(out=ps[:], lhsT=ones[:], rhs=brow[:, q * 512 : (q + 1) * 512], start=True, stop=True)
-            nc.vector.tensor_copy(out=bias[:, q * 512 : (q + 1) * 512], in_=ps[:])
+
+        def spread_bias():
+            for q in range(4):
+                ps = bank()
+                nc.tensor.matmul(out=ps[:], lhsT=ones[:], rhs=brow[:, q * 512 : (q + 1) * 512], start=True, stop=True)
+                if q % 2 == 0:
+                    nc.vector.tensor_copy(out=bias[:, q * 512 : (q + 1) * 512], in_=ps[:])
+                else:
+                    nc.scalar.copy(out=bias[:, q * 512 : (q + 1) * 512], in_=ps[:])
 
         wc = [const.tile([P, N], U32, name="wc%d" % o, align_bytes=64) for o in range(2)]
         wsc = [const.tile([P, N], U8, name="wsc%d" % o, align_bytes=64) for o in range(2)]
+        wgs = {}
 
-        def prep_w(o, hf):
+        def w_transpose(o, hf, second_on_vector):
             raw_w = wraw[o][hf][:].bitcast(F32)
             wg = wgp.tile([P, 2048], BF16, tag="wg", name="wg", align_bytes=64)
             wg_w = wg[:].bitcast(F32)
             for pr in range(2):
-                tp = tpp.tile([P, 4, P], F32, tag="tp", name="tp")
-                for jj in range(2):
-                    for u in range(2):
-                        c0 = (2 * pr + jj) * 256 + u * 128
-                        nc.tensor.transpose(tp[:, 2 * jj + u, :], raw_w[:, c0 : c0 + 128], ident[:])
+                tp = bank()
+                for q in range(4):
+                    c0 = pr * 512 + q * 128
+                    nc.tensor.transpose(tp[:, q * P : (q + 1) * P], raw_w[:, c0 : c0 + 128], ident[:])
                 dst = wg_w[:, pr * 512 : (pr + 1) * 512].rearrange("p (a r u) -> p a r u", a=2, u=2)
-                src = tp[:].rearrange("p (a u) r -> p a r u", u=2)
-                if pr == 0:
+                src = tp[:].rearrange("p (a u r) -> p a r u", a=2, u=2)
+                if pr == 1 and second_on_vector:
                     nc.vector.tensor_copy(out=dst, in_=src)
                 else:
                     nc.scalar.copy(out=dst, in_=src)
+            wgs[(o, hf)] = wg
+
+        def w_quantise(o, hf):
             cols = slice(hf * 512, (hf + 1) * 512)
-            nc.vector.quantize_mx(out=wc[o][:, cols].bitcast(FP8X4), scales=wsc[o][:, cols], in_=wg[:])
+            nc.vector.quantize_mx(out=wc[o][:, cols].bitcast(FP8X4), scales=wsc[o][:, cols], in_=wgs[(o, hf)][:])
 
         def act_words(o, t):
             for ci in range(len(CHUNKS)):
@@ -120,110 +131,190 @@ def tile_layernormgrucell_pa_t_kernel(tc, x, h, W_irz, b_irz, W_hrz, b_hrz, out)
                     return xch[o][ci][:].bitcast(F32)[:, (t - t0) * 256 : (t - t0 + 1) * 256]
             raise ValueError("no chunk")
 
-        def stage_a(g):
-            xg = xgp.tile([P, T * 1024], BF16, tag="xg", name="xg", align_bytes=64)
-            xg_w = xg[:].bitcast(F32)
-            for tt in range(T):
-                tp = tpp.tile([P, 4, P], F32, tag="tp", name="tp")
-                for o in range(2):
-                    w_ = act_words(o, g * T + tt)
-                    for u in range(2):
-                        nc.tensor.transpose(tp[:, 2 * o + u, :], w_[:, u * 128 : (u + 1) * 128], ident[:])
-                dst = xg_w[:, tt * 512 : (tt + 1) * 512].rearrange("p (a r u) -> p a r u", a=2, u=2)
-                nc.scalar.copy(out=dst, in_=tp[:].rearrange("p (a u) r -> p a r u", u=2))
-            xc = xcp.tile([P, T * 256], U32, tag="xc", name="xc", align_bytes=64)
-            xs = xcp.tile([P, T * 256], U8, tag="xs", name="xs", align_bytes=64)
-            nc.vector.quantize_mx(out=xc[:].bitcast(FP8X4), scales=xs[:], in_=xg[:])
-            return xc, xs
+        tps = {}
+        xgs = {}
+        xcs = {}
+        pss = {}
+        abs_ = {}
+        sts = {}
 
-        def stage_b(g, xc, xs):
-            ab = abp.tile([P, T, 2, N], F32, tag="ab", name="ab")
-            sv = stp.tile([P, 2, 2 * T], F32, tag="sv", name="sv")
-            for tt in range(T):
-                for o in range(2):
-                    i = tt * 2 + o
-                    for hf in range(2):
-                        cols = slice(hf * 512, (hf + 1) * 512)
-                        ps = mmp.tile([P, 512], F32, tag="mm", name="ps")
-                        nc.tensor.matmul_mx(
-                            out=ps[:],
-                            lhsT=xc[:, i * P : (i + 1) * P].bitcast(FP8X4),
-                            lhsT_scale=xs[:, i * P : (i + 1) * P],
-                            rhs=wc[o][:, cols].bitcast(FP8X4),
-                            rhs_scale=wsc[o][:, cols],
-                            start=True,
-                            stop=True,
-                        )
-                        nc.vector.scalar_tensor_tensor(
-                            out=ab[:, tt, o, cols],
-                            in0=ps[:],
-                            scalar=1.0,
-                            in1=bias[:, o * N + hf * 512 : o * N + (hf + 1) * 512],
-                            op0=ALU.mult,
-                            op1=ALU.add,
-                            accum_out=sv[:, hf, i : i + 1],
-                        )
-            sm = stp.tile([P, 2 * T], F32, tag="sm", name="sm")
-            nc.vector.tensor_tensor(out=sm[:], in0=sv[:, 0, :], in1=sv[:, 1, :], op=ALU.add)
-            negmu = stp.tile([P, 2 * T], F32, tag="negmu", name="negmu")
-            nc.vector.tensor_scalar(out=negmu[:], in0=sm[:], scalar1=-1.0 / N, scalar2=None, op0=ALU.mult)
-            ss = stp.tile([P, 2 * T], F32, tag="ss", name="ss")
-            for i in range(2 * T):
-                junk = jp.tile([P, N], BF16, tag="junk", name="junk")
-                nc.scalar.activation(
-                    out=junk[:],
-                    in_=ab[:, i // 2, i % 2, :],
-                    func=ACT.Square,
-                    bias=negmu[:, i : i + 1],
-                    scale=1.0,
-                    accum_out=ss[:, i : i + 1],
+        def ok(t):
+            return 0 <= t < NT
+
+        def on_gpsimd(t):
+            return GP5 > 0 and t % GP5 == GP5 - 1 and t < NT - 2
+
+        def s_tr(t):
+            tp = bank()
+            for o in range(2):
+                w_ = act_words(o, t)
+                for u in range(2):
+                    q = 2 * o + u
+                    nc.tensor.transpose(tp[:, q * P : (q + 1) * P], w_[:, u * 128 : (u + 1) * 128], ident[:])
+            tps[t] = tp
+
+        def s_ev(t):
+            xg = xgp.tile([P, 1024], BF16, tag="xg", name="xg", align_bytes=64)
+            dst = xg[:].bitcast(F32).rearrange("p (a r u) -> p a r u", a=2, u=2)
+            src = tps[t][:].rearrange("p (a u r) -> p a r u", a=2, u=2)
+            if EV_ON_VECTOR > 0 and t % EV_ON_VECTOR == 0 and t >= 3:
+                nc.vector.tensor_copy(out=dst, in_=src)
+            else:
+                nc.scalar.copy(out=dst, in_=src)
+            xgs[t] = xg
+
+        def s_q(t):
+            xc = xcp.tile([P, 256], U32, tag="xc", name="xc", align_bytes=64)
+            xs = xcp.tile([P, 256], U8, tag="xs", name="xs", align_bytes=64)
+            nc.vector.quantize_mx(out=xc[:].bitcast(FP8X4), scales=xs[:], in_=xgs[t][:])
+            xcs[t] = (xc, xs)
+
+        def s_mx(t, o, hf):
+            xc, xs = xcs[t]
+            cols = slice(hf * 512, (hf + 1) * 512)
+            ps = bank()
+            nc.tensor.matmul_mx(
+                out=ps[:],
+                lhsT=xc[:, o * P : (o + 1) * P].bitcast(FP8X4),
+                lhsT_scale=xs[:, o * P : (o + 1) * P],
+                rhs=wc[o][:, cols].bitcast(FP8X4),
+                rhs_scale=wsc[o][:, cols],
+                start=True,
+                stop=True,
+            )
+            pss[(t, o, hf)] = ps
+
+        def s_p1(t, o, hf):
+            if (o, hf) == (0, 0):
+                abs_[t] = abp.tile([P, 2, N], F32, tag="ab", name="ab")
+                sts[t] = {
+                    "sv": stp.tile([P, 2, 2], F32, tag="sv", name="sv"),
+                    "negmu": stp.tile([P, 2], F32, tag="negmu", name="negmu"),
+                    "ss": stp.tile([P, 2], F32, tag="ss", name="ss"),
+                }
+            nc.vector.scalar_tensor_tensor(
+                out=abs_[t][:, o, hf * 512 : (hf + 1) * 512],
+                in0=pss[(t, o, hf)][:],
+                scalar=1.0,
+                in1=bias[:, o * N + hf * 512 : o * N + (hf + 1) * 512],
+                op0=ALU.mult,
+                op1=ALU.add,
+                accum_out=sts[t]["sv"][:, o, hf : hf + 1],
+            )
+            if hf == 1:
+                nc.vector.tensor_scalar(
+                    out=sts[t]["negmu"][:, o : o + 1],
+                    in0=sts[t]["sv"][:, o, 0:1],
+                    scalar1=sts[t]["sv"][:, o, 1:2],
+                    scalar2=-1.0 / N,
+                    op0=ALU.add,
+                    op1=ALU.mult,
                 )
-            return ab, negmu, ss
 
-        def stage_c(g, ab, negmu, ss):
-            ve = stp.tile([P, 2 * T], F32, tag="ve", name="ve")
-            nc.gpsimd.tensor_scalar(out=ve[:], in0=ss[:], scalar1=1.0 / N, scalar2=EPS, op0=ALU.mult, op1=ALU.add)
-            rs = stp.tile([P, 2 * T], F32, tag="rs", name="rs")
+        def s_sq(t, o):
+            junk = jp.tile([P, N], BF16, tag="junk", name="junk")
+            nc.scalar.activation(
+                out=junk[:],
+                in_=abs_[t][:, o, :],
+                func=ACT.Square,
+                bias=sts[t]["negmu"][:, o : o + 1],
+                scale=1.0,
+                accum_out=sts[t]["ss"][:, o : o + 1],
+            )
+
+        def s_ch(t):
+            st = sts[t]
+            ve = stp.tile([P, 2], F32, tag="ve", name="ve")
+            nc.gpsimd.tensor_scalar(out=ve[:], in0=st["ss"][:], scalar1=1.0 / N, scalar2=EPS, op0=ALU.mult, op1=ALU.add)
+            rs = stp.tile([P, 2], F32, tag="rs", name="rs")
             nc.gpsimd.tensor_tensor(out=rs[:], in0=ve[:], in1=mhalf[:], op=ALU.pow)
-            ve_v = ve[:].rearrange("p (t o) -> p t o", o=2)
-            rs_v = rs[:].rearrange("p (t o) -> p t o", o=2)
-            sd = stp.tile([P, T], F32, tag="sd", name="sd")
-            nc.gpsimd.tensor_tensor(out=sd[:], in0=ve_v[:, :, 1], in1=rs_v[:, :, 1], op=ALU.mult)
-            rho = stp.tile([P, T], F32, tag="rho", name="rho")
-            nc.gpsimd.tensor_tensor(out=rho[:], in0=sd[:], in1=rs_v[:, :, 0], op=ALU.mult)
-            m = stp.tile([P, 2 * T], F32, tag="m", name="m")
-            nc.gpsimd.tensor_tensor(out=m[:], in0=negmu[:], in1=rs[:], op=ALU.mult)
-            m_v = m[:].rearrange("p (t o) -> p t o", o=2)
-            c = stp.tile([P, T], F32, tag="c", name="c")
-            nc.gpsimd.tensor_tensor(out=c[:], in0=m_v[:, :, 0], in1=m_v[:, :, 1], op=ALU.add)
-            ot = op.tile([P, T, N], F32, tag="ot", name="ot")
-            for tt in range(T):
+            sd = stp.tile([P, 1], F32, tag="sd", name="sd")
+            nc.gpsimd.tensor_tensor(out=sd[:], in0=ve[:, 1:2], in1=rs[:, 1:2], op=ALU.mult)
+            rho = stp.tile([P, 1], F32, tag="rho", name="rho")
+            nc.gpsimd.tensor_tensor(out=rho[:], in0=sd[:], in1=rs[:, 0:1], op=ALU.mult)
+            m = stp.tile([P, 2], F32, tag="m", name="m")
+            nc.gpsimd.tensor_tensor(out=m[:], in0=st["negmu"][:], in1=rs[:], op=ALU.mult)
+            c = stp.tile([P, 1], F32, tag="c", name="c")
+            nc.gpsimd.tensor_tensor(out=c[:], in0=m[:, 0:1], in1=m[:, 1:2], op=ALU.add)
+            st["rs"] = rs
+            st["rho"] = rho
+            st["c"] = c
+
+        def s_p5(t):
+            ab = abs_[t]
+            if on_gpsimd(t):
+                nc.gpsimd.tensor_scalar(
+                    out=ab[:, 0, :], in0=ab[:, 0, :], scalar1=sts[t]["rho"][:], scalar2=0.0, op0=ALU.mult, op1=ALU.add
+                )
+                nc.gpsimd.tensor_tensor(out=ab[:, 1, :], in0=ab[:, 0, :], in1=ab[:, 1, :], op=ALU.add)
+            else:
                 nc.vector.scalar_tensor_tensor(
-                    out=ab[:, tt, 1, :],
-                    in0=ab[:, tt, 0, :],
-                    scalar=rho[:, tt : tt + 1],
-                    in1=ab[:, tt, 1, :],
+                    out=ab[:, 1, :],
+                    in0=ab[:, 0, :],
+                    scalar=sts[t]["rho"][:],
+                    in1=ab[:, 1, :],
                     op0=ALU.mult,
                     op1=ALU.add,
                 )
-                nc.scalar.activation(
-                    out=ot[:, tt, :],
-                    in_=ab[:, tt, 1, :],
-                    func=ACT.Sigmoid,
-                    bias=c[:, tt : tt + 1],
-                    scale=rs[:, 2 * tt + 1 : 2 * tt + 2],
-                )
-            nc.sync.dma_start(
-                out=out.rearrange("(p t) j -> p t j", t=NT)[:, g * T : (g + 1) * T, :],
-                in_=ot[:],
-            )
 
-        prep_w(0, 0)
-        q0 = stage_a(0)
-        prep_w(0, 1)
-        prep_w(1, 0)
-        prep_w(1, 1)
-        for g in range(NG):
-            xc, xs = q0 if g == 0 else stage_a(g)
-            ab, negmu, ss = stage_b(g, xc, xs)
-            stage_c(g, ab, negmu, ss)
+        def s_sig(t):
+            ot = op.tile([P, N], F32, tag="ot", name="ot")
+            nc.scalar.activation(
+                out=ot[:],
+                in_=abs_[t][:, 1, :],
+                func=ACT.Sigmoid,
+                bias=sts[t]["c"][:],
+                scale=sts[t]["rs"][:, 1:2],
+            )
+            nc.sync.dma_start(out=out.rearrange("(p t) j -> p t j", t=NT)[:, t, :], in_=ot[:])
+
+        w_transpose(0, 0, True)
+        w_quantise(0, 0)
+        s_tr(0)
+        s_ev(0)
+        s_q(0)
+        spread_bias()
+        w_transpose(0, 1, False)
+        s_mx(0, 0, 0)
+        s_p1(0, 0, 0)
+        w_quantise(0, 1)
+        w_transpose(1, 0, False)
+        s_mx(0, 0, 1)
+        s_p1(0, 0, 1)
+        w_quantise(1, 0)
+        w_transpose(1, 1, False)
+        s_mx(0, 1, 0)
+        s_p1(0, 1, 0)
+        s_sq(0, 0)
+        w_quantise(1, 1)
+        s_tr(1)
+        s_ev(1)
+        s_mx(0, 1, 1)
+        s_p1(0, 1, 1)
+        s_tr(2)
+        s_ev(2)
+
+        for it in range(NT + LAG):
+            if ok(it) and it > 0:
+                for o in range(2):
+                    for hf in range(2):
+                        s_p1(it, o, hf)
+            if ok(it + 1):
+                s_q(it + 1)
+                for o in range(2):
+                    for hf in range(2):
+                        s_mx(it + 1, o, hf)
+            if ok(it + 3):
+                s_tr(it + 3)
+            if ok(it - 1):
+                s_ch(it - 1)
+            if ok(it - 2):
+                s_p5(it - 2)
+            if ok(it):
+                if it > 0:
+                    s_sq(it, 0)
+                s_sq(it, 1)
+            if ok(it - LAG):
+                s_sig(it - LAG)
+            if ok(it + 3):
+                s_ev(it + 3)

@@ -20,10 +20,11 @@ EPS = 1e-5
 FLOPS = 2 * 2 * B * K * N
 CHUNKS = [(0, 2), (2, 6), (8, 8), (16, 8), (24, 8)]
 
-EV_ON_VECTOR = 0
-LAG = 2
-GP5 = 0
-AB_BUFS = 5
+EV_ON_SCALAR = 3
+LAG = 5
+GP5 = 3
+HEAD = 2
+AB_BUFS = 8
 
 
 def tile_layernormgrucell_pa_t_kernel(tc, x, h, W_irz, b_irz, W_hrz, b_hrz, out):
@@ -49,7 +50,7 @@ def tile_layernormgrucell_pa_t_kernel(tc, x, h, W_irz, b_irz, W_hrz, b_hrz, out)
         nc.vector.memset(brow[:].bitcast(mybir.dt.int32), 0)
         ones = const.tile([P, P], BF16, name="ones")
         nc.vector.memset(ones[:], 1.0)
-        mhalf = const.tile([P, 2], F32, name="mhalf")
+        mhalf = const.tile([P, 4], F32, name="mhalf")
         nc.vector.memset(mhalf[:], -0.5)
         warm = const.tile([P, 1], F32, name="warm")
         nc.scalar.activation(out=warm[:], in_=mhalf[:, 0:1], func=ACT.Sigmoid)
@@ -142,7 +143,7 @@ def tile_layernormgrucell_pa_t_kernel(tc, x, h, W_irz, b_irz, W_hrz, b_hrz, out)
             return 0 <= t < NT
 
         def on_gpsimd(t):
-            return GP5 > 0 and t % GP5 == GP5 - 1 and t < NT - 2
+            return GP5 > 0 and t % GP5 == GP5 - 1 and t < NT - 4
 
         def s_tr(t):
             tp = bank()
@@ -157,7 +158,7 @@ def tile_layernormgrucell_pa_t_kernel(tc, x, h, W_irz, b_irz, W_hrz, b_hrz, out)
             xg = xgp.tile([P, 1024], BF16, tag="xg", name="xg", align_bytes=64)
             dst = xg[:].bitcast(F32).rearrange("p (a r u) -> p a r u", a=2, u=2)
             src = tps[t][:].rearrange("p (a u r) -> p a r u", a=2, u=2)
-            if EV_ON_VECTOR > 0 and t % EV_ON_VECTOR == 0 and t >= 3:
+            if t % EV_ON_SCALAR != 0 and t >= 3:
                 nc.vector.tensor_copy(out=dst, in_=src)
             else:
                 nc.scalar.copy(out=dst, in_=src)
@@ -187,74 +188,84 @@ def tile_layernormgrucell_pa_t_kernel(tc, x, h, W_irz, b_irz, W_hrz, b_hrz, out)
         def s_p1(t, o, hf):
             if (o, hf) == (0, 0):
                 abs_[t] = abp.tile([P, 2, N], F32, tag="ab", name="ab")
-                sts[t] = {
-                    "sv": stp.tile([P, 2, 2], F32, tag="sv", name="sv"),
-                    "negmu": stp.tile([P, 2], F32, tag="negmu", name="negmu"),
-                    "ss": stp.tile([P, 2], F32, tag="ss", name="ss"),
-                }
+                if t % 2 == 0:
+                    sts[t // 2] = {
+                        "sv": stp.tile([P, 2, 4], F32, tag="sv", name="sv"),
+                        "ss": stp.tile([P, 4], F32, tag="ss", name="ss"),
+                    }
+            i = (t % 2) * 2 + o
             nc.vector.scalar_tensor_tensor(
                 out=abs_[t][:, o, hf * 512 : (hf + 1) * 512],
                 in0=pss[(t, o, hf)][:],
-                scalar=1.0,
+                scalar=-1.0,
                 in1=bias[:, o * N + hf * 512 : o * N + (hf + 1) * 512],
                 op0=ALU.mult,
-                op1=ALU.add,
-                accum_out=sts[t]["sv"][:, o, hf : hf + 1],
+                op1=ALU.subtract,
+                accum_out=sts[t // 2]["sv"][:, hf, i : i + 1],
             )
-            if hf == 1:
-                nc.vector.tensor_scalar(
-                    out=sts[t]["negmu"][:, o : o + 1],
-                    in0=sts[t]["sv"][:, o, 0:1],
-                    scalar1=sts[t]["sv"][:, o, 1:2],
-                    scalar2=-1.0 / N,
-                    op0=ALU.add,
-                    op1=ALU.mult,
-                )
 
         def s_sq(t, o):
+            i = (t % 2) * 2 + o
             junk = jp.tile([P, N], BF16, tag="junk", name="junk")
             nc.scalar.activation(
                 out=junk[:],
                 in_=abs_[t][:, o, :],
                 func=ACT.Square,
-                bias=sts[t]["negmu"][:, o : o + 1],
-                scale=1.0,
-                accum_out=sts[t]["ss"][:, o : o + 1],
+                bias=sts[t // 2]["sv"][:, 0, i : i + 1],
+                scale=-512.0,
+                accum_out=sts[t // 2]["ss"][:, i : i + 1],
             )
 
-        def s_ch(t):
-            st = sts[t]
-            ve = stp.tile([P, 2], F32, tag="ve", name="ve")
-            nc.gpsimd.tensor_scalar(out=ve[:], in0=st["ss"][:], scalar1=1.0 / N, scalar2=EPS, op0=ALU.mult, op1=ALU.add)
-            rs = stp.tile([P, 2], F32, tag="rs", name="rs")
-            nc.gpsimd.tensor_tensor(out=rs[:], in0=ve[:], in1=mhalf[:], op=ALU.pow)
-            sd = stp.tile([P, 1], F32, tag="sd", name="sd")
-            nc.gpsimd.tensor_tensor(out=sd[:], in0=ve[:, 1:2], in1=rs[:, 1:2], op=ALU.mult)
-            rho = stp.tile([P, 1], F32, tag="rho", name="rho")
-            nc.gpsimd.tensor_tensor(out=rho[:], in0=sd[:], in1=rs[:, 0:1], op=ALU.mult)
-            m = stp.tile([P, 2], F32, tag="m", name="m")
-            nc.gpsimd.tensor_tensor(out=m[:], in0=st["negmu"][:], in1=rs[:], op=ALU.mult)
-            c = stp.tile([P, 1], F32, tag="c", name="c")
-            nc.gpsimd.tensor_tensor(out=c[:], in0=m[:, 0:1], in1=m[:, 1:2], op=ALU.add)
-            st["rs"] = rs
+        def small(name, width):
+            return stp.tile([P, width], F32, tag=name, name=name)
+
+        def s_ch(m_):
+            st = sts[m_]
+            s0 = st["sv"][:, 0, :]
+            s1 = st["sv"][:, 1, :]
+            tt = nc.gpsimd.tensor_tensor
+            dd = small("dd", 4)
+            tt(out=dd[:], in0=s1, in1=s0, op=ALU.subtract)
+            d2 = small("d2", 4)
+            tt(out=d2[:], in0=dd[:], in1=dd[:], op=ALU.mult)
+            sm = small("sm", 4)
+            tt(out=sm[:], in0=s0, in1=s1, op=ALU.add)
+            qq = small("qq", 4)
+            nc.gpsimd.tensor_scalar(
+                out=qq[:], in0=st["ss"][:], scalar1=1.0 / 256.0, scalar2=EPS * N * N, op0=ALU.mult, op1=ALU.add
+            )
+            vn = small("vn", 4)
+            tt(out=vn[:], in0=qq[:], in1=d2[:], op=ALU.subtract)
+            rsn = small("rsn", 4)
+            tt(out=rsn[:], in0=vn[:], in1=mhalf[:], op=ALU.pow)
+            vn_v = vn[:].rearrange("p (t o) -> p t o", o=2)
+            rsn_v = rsn[:].rearrange("p (t o) -> p t o", o=2)
+            sdn = small("sdn", 2)
+            tt(out=sdn[:], in0=vn_v[:, :, 1], in1=rsn_v[:, :, 1], op=ALU.mult)
+            rho = small("rho", 2)
+            tt(out=rho[:], in0=sdn[:], in1=rsn_v[:, :, 0], op=ALU.mult)
+            mm_ = small("mm_", 4)
+            tt(out=mm_[:], in0=sm[:], in1=rsn[:], op=ALU.mult)
+            mm_v = mm_[:].rearrange("p (t o) -> p t o", o=2)
+            c = small("c", 2)
+            tt(out=c[:], in0=mm_v[:, :, 0], in1=mm_v[:, :, 1], op=ALU.add)
+            nsc = small("nsc", 2)
+            nc.gpsimd.tensor_scalar(
+                out=nsc[:], in0=rsn_v[:, :, 1], scalar1=-1.0 * N, scalar2=0.0, op0=ALU.mult, op1=ALU.add
+            )
             st["rho"] = rho
             st["c"] = c
+            st["nsc"] = nsc
 
         def s_p5(t):
             ab = abs_[t]
+            rho = sts[t // 2]["rho"][:, t % 2 : t % 2 + 1]
             if on_gpsimd(t):
-                nc.gpsimd.tensor_scalar(
-                    out=ab[:, 0, :], in0=ab[:, 0, :], scalar1=sts[t]["rho"][:], scalar2=0.0, op0=ALU.mult, op1=ALU.add
-                )
+                nc.gpsimd.tensor_scalar(out=ab[:, 0, :], in0=ab[:, 0, :], scalar1=rho, scalar2=0.0, op0=ALU.mult, op1=ALU.add)
                 nc.gpsimd.tensor_tensor(out=ab[:, 1, :], in0=ab[:, 0, :], in1=ab[:, 1, :], op=ALU.add)
             else:
                 nc.vector.scalar_tensor_tensor(
-                    out=ab[:, 1, :],
-                    in0=ab[:, 0, :],
-                    scalar=sts[t]["rho"][:],
-                    in1=ab[:, 1, :],
-                    op0=ALU.mult,
-                    op1=ALU.add,
+                    out=ab[:, 1, :], in0=ab[:, 0, :], scalar=rho, in1=ab[:, 1, :], op0=ALU.mult, op1=ALU.add
                 )
 
         def s_sig(t):
@@ -263,55 +274,56 @@ def tile_layernormgrucell_pa_t_kernel(tc, x, h, W_irz, b_irz, W_hrz, b_hrz, out)
                 out=ot[:],
                 in_=abs_[t][:, 1, :],
                 func=ACT.Sigmoid,
-                bias=sts[t]["c"][:],
-                scale=sts[t]["rs"][:, 1:2],
+                bias=sts[t // 2]["c"][:, t % 2 : t % 2 + 1],
+                scale=sts[t // 2]["nsc"][:, t % 2 : t % 2 + 1],
             )
             nc.sync.dma_start(out=out.rearrange("(p t) j -> p t j", t=NT)[:, t, :], in_=ot[:])
 
         w_transpose(0, 0, True)
         w_quantise(0, 0)
-        s_tr(0)
-        s_ev(0)
-        s_q(0)
+        for t in range(HEAD):
+            s_tr(t)
+            s_ev(t)
+            s_q(t)
         spread_bias()
         w_transpose(0, 1, False)
-        s_mx(0, 0, 0)
-        s_p1(0, 0, 0)
-        w_quantise(0, 1)
-        w_transpose(1, 0, False)
-        s_mx(0, 0, 1)
-        s_p1(0, 0, 1)
-        w_quantise(1, 0)
-        w_transpose(1, 1, False)
-        s_mx(0, 1, 0)
-        s_p1(0, 1, 0)
-        s_sq(0, 0)
-        w_quantise(1, 1)
-        s_tr(1)
-        s_ev(1)
-        s_mx(0, 1, 1)
-        s_p1(0, 1, 1)
-        s_tr(2)
-        s_ev(2)
+        for (o, hf) in ((0, 0), (0, 1), (1, 0), (1, 1)):
+            for t in range(HEAD):
+                s_mx(t, o, hf)
+            for t in range(HEAD):
+                s_p1(t, o, hf)
+            if (o, hf) == (0, 0):
+                w_quantise(0, 1)
+                w_transpose(1, 0, False)
+            if (o, hf) == (0, 1):
+                w_quantise(1, 0)
+                w_transpose(1, 1, False)
+            if (o, hf) == (1, 0):
+                w_quantise(1, 1)
+                for t in range(HEAD):
+                    s_sq(t, 0)
+                s_tr(2)
+                s_ev(2)
+        s_tr(3)
 
         for it in range(NT + LAG):
-            if ok(it) and it > 0:
+            if ok(it) and it >= HEAD:
                 for o in range(2):
                     for hf in range(2):
                         s_p1(it, o, hf)
-            if ok(it + 1):
+            if ok(it + 1) and it + 1 >= HEAD:
                 s_q(it + 1)
                 for o in range(2):
                     for hf in range(2):
                         s_mx(it + 1, o, hf)
-            if ok(it + 3):
-                s_tr(it + 3)
-            if ok(it - 1):
-                s_ch(it - 1)
-            if ok(it - 2):
-                s_p5(it - 2)
+            if ok(it + 4):
+                s_tr(it + 4)
+            if it % 2 == 0 and ok(it - 2):
+                s_ch((it - 2) // 2)
+            if ok(it - 3):
+                s_p5(it - 3)
             if ok(it):
-                if it > 0:
+                if it >= HEAD:
                     s_sq(it, 0)
                 s_sq(it, 1)
             if ok(it - LAG):

@@ -20,11 +20,10 @@ EPS = 1e-5
 FLOPS = 2 * 2 * B * K * N
 CHUNKS = [(0, 2), (2, 6), (8, 8), (16, 8), (24, 8)]
 
-EV_ON_SCALAR = 3
-LAG = 5
-GP5 = 3
+LAG = 3
+GP5 = 0
 HEAD = 2
-AB_BUFS = 8
+AB_BUFS = 6
 
 
 def tile_layernormgrucell_pa_t_kernel(tc, x, h, W_irz, b_irz, W_hrz, b_hrz, out):
@@ -158,7 +157,7 @@ def tile_layernormgrucell_pa_t_kernel(tc, x, h, W_irz, b_irz, W_hrz, b_hrz, out)
             xg = xgp.tile([P, 1024], BF16, tag="xg", name="xg", align_bytes=64)
             dst = xg[:].bitcast(F32).rearrange("p (a r u) -> p a r u", a=2, u=2)
             src = tps[t][:].rearrange("p (a u r) -> p a r u", a=2, u=2)
-            if t % EV_ON_SCALAR != 0 and t >= 3:
+            if (t % 3 == 0) and t >= 3:
                 nc.vector.tensor_copy(out=dst, in_=src)
             else:
                 nc.scalar.copy(out=dst, in_=src)

@@ -20,10 +20,10 @@ EPS = 1e-5
 FLOPS = 2 * 2 * B * K * N
 CHUNKS = [(0, 2), (2, 6), (8, 8), (16, 8), (24, 8)]
 
-LAG = 3
+LAG = 5
 GP5 = 0
 HEAD = 2
-AB_BUFS = 6
+AB_BUFS = 8
 
 
 def tile_layernormgrucell_pa_t_kernel(tc, x, h, W_irz, b_irz, W_hrz, b_hrz, out):
@@ -319,8 +319,8 @@ def tile_layernormgrucell_pa_t_kernel(tc, x, h, W_irz, b_irz, W_hrz, b_hrz, out)
                 s_tr(it + 4)
             if it % 2 == 0 and ok(it - 2):
                 s_ch((it - 2) // 2)
-            if ok(it - 3):
-                s_p5(it - 3)
+            if ok(it - LAG):
+                s_p5(it - LAG)
             if ok(it):
                 if it >= HEAD:
                     s_sq(it, 0)

@@ -18,7 +18,7 @@ N = 1024
 NT = B // P
 EPS = 1e-5
 FLOPS = 2 * 2 * B * K * N
-CHUNKS = [(0, 2), (2, 6), (8, 8), (16, 8), (24, 8)]
+CHUNKS = [(0, 2), (2, 2), (4, 4), (8, 8), (16, 8), (24, 8)]
 
 LAG = 5
 GP5 = 0
@@ -32,7 +32,7 @@ def tile_layernormgrucell_pa_t_kernel(tc, x, h, W_irz, b_irz, W_hrz, b_hrz, out)
         const = ctx.enter_context(tc.tile_pool(name="const", bufs=1))
         wgp = ctx.enter_context(tc.tile_pool(name="wgp", bufs=2))
         xgp = ctx.enter_context(tc.tile_pool(name="xgp", bufs=3))
-        xcp = ctx.enter_context(tc.tile_pool(name="xcp", bufs=2))
+        xcp = ctx.enter_context(tc.tile_pool(name="xcp", bufs=3))
         abp = ctx.enter_context(tc.tile_pool(name="abp", bufs=AB_BUFS))
         op = ctx.enter_context(tc.tile_pool(name="op", bufs=4))
         jp = ctx.enter_context(tc.tile_pool(name="jp", bufs=2))
@@ -157,7 +157,7 @@ def tile_layernormgrucell_pa_t_kernel(tc, x, h, W_irz, b_irz, W_hrz, b_hrz, out)
             xg = xgp.tile([P, 1024], BF16, tag="xg", name="xg", align_bytes=64)
             dst = xg[:].bitcast(F32).rearrange("p (a r u) -> p a r u", a=2, u=2)
             src = tps[t][:].rearrange("p (a u r) -> p a r u", a=2, u=2)
-            if (t % 3 == 0) and t >= 3:
+            if (t % 3 == 0) and t >= 4:
                 nc.vector.tensor_copy(out=dst, in_=src)
             else:
                 nc.scalar.copy(out=dst, in_=src)
@@ -301,22 +301,25 @@ def tile_layernormgrucell_pa_t_kernel(tc, x, h, W_irz, b_irz, W_hrz, b_hrz, out)
                 w_quantise(1, 1)
                 for t in range(HEAD):
                     s_sq(t, 0)
-                s_tr(2)
-                s_ev(2)
-        s_tr(3)
+                for t in (2, 3):
+                    s_tr(t)
+                    s_ev(t)
+        s_q(2)
+        s_tr(4)
 
         for it in range(NT + LAG):
+            if ok(it + 2) and it + 2 > HEAD:
+                s_q(it + 2)
             if ok(it) and it >= HEAD:
                 for o in range(2):
                     for hf in range(2):
                         s_p1(it, o, hf)
             if ok(it + 1) and it + 1 >= HEAD:
-                s_q(it + 1)
                 for o in range(2):
                     for hf in range(2):
                         s_mx(it + 1, o, hf)
-            if ok(it + 4):
-                s_tr(it + 4)
+            if ok(it + 5):
+                s_tr(it + 5)
             if it % 2 == 0 and ok(it - 2):
                 s_ch((it - 2) // 2)
             if ok(it - LAG):
@@ -327,5 +330,5 @@ def tile_layernormgrucell_pa_t_kernel(tc, x, h, W_irz, b_irz, W_hrz, b_hrz, out)
                 s_sq(it, 1)
             if ok(it - LAG):
                 s_sig(it - LAG)
-            if ok(it + 3):
-                s_ev(it + 3)
+            if ok(it + 4):
+                s_ev(it + 4)

@@ -23,6 +23,7 @@ CHUNKS = [(0, 2), (2, 2), (4, 4), (8, 8), (16, 8), (24, 8)]
 LAG = 5
 GP5 = 0
 HEAD = 2
+PEJ = 3
 AB_BUFS = 8
 
 
@@ -37,6 +38,7 @@ def tile_layernormgrucell_pa_t_kernel(tc, x, h, W_irz, b_irz, W_hrz, b_hrz, out)
         op = ctx.enter_context(tc.tile_pool(name="op", bufs=4))
         jp = ctx.enter_context(tc.tile_pool(name="jp", bufs=2))
         stp = ctx.enter_context(tc.tile_pool(name="stp", bufs=AB_BUFS + 2))
+        dgp = ctx.enter_context(tc.tile_pool(name="dgp", bufs=2))
         psp = ctx.enter_context(tc.psum_pool(name="psp", bufs=8))
         ctx.enter_context(tc.manual_schedule())
 
@@ -131,6 +133,7 @@ def tile_layernormgrucell_pa_t_kernel(tc, x, h, W_irz, b_irz, W_hrz, b_hrz, out)
                     return xch[o][ci][:].bitcast(F32)[:, (t - t0) * 256 : (t - t0 + 1) * 256]
             raise ValueError("no chunk")
 
+        dgs = {}
         tps = {}
         xgs = {}
         xcs = {}
@@ -256,6 +259,25 @@ def tile_layernormgrucell_pa_t_kernel(tc, x, h, W_irz, b_irz, W_hrz, b_hrz, out)
             st["c"] = c
             st["nsc"] = nsc
 
+        def on_tensor(t):
+            return PEJ > 0 and t % PEJ == PEJ - 1
+
+        def s_diag(t):
+            dg = dgp.tile([P, P], F32, tag="dg", name="dg")
+            nc.gpsimd.tensor_scalar(
+                out=dg[:], in0=ident[:], scalar1=sts[t // 2]["rho"][:, t % 2 : t % 2 + 1], scalar2=0.0, op0=ALU.mult, op1=ALU.add
+            )
+            dgs[t] = dg
+
+        def s_join_pe(t):
+            ab = abs_[t]
+            for hf in range(2):
+                cols = slice(hf * 512, (hf + 1) * 512)
+                ps = bank()
+                nc.tensor.matmul(out=ps[:], lhsT=dgs[t][:], rhs=ab[:, 0, cols], start=True, stop=False)
+                nc.tensor.matmul(out=ps[:], lhsT=ident[:], rhs=ab[:, 1, cols], start=False, stop=True)
+                pss[("j", t, hf)] = ps
+
         def s_p5(t):
             ab = abs_[t]
             rho = sts[t // 2]["rho"][:, t % 2 : t % 2 + 1]
@@ -269,13 +291,15 @@ def tile_layernormgrucell_pa_t_kernel(tc, x, h, W_irz, b_irz, W_hrz, b_hrz, out)
 
         def s_sig(t):
             ot = op.tile([P, N], F32, tag="ot", name="ot")
-            nc.scalar.activation(
-                out=ot[:],
-                in_=abs_[t][:, 1, :],
-                func=ACT.Sigmoid,
-                bias=sts[t // 2]["c"][:, t % 2 : t % 2 + 1],
-                scale=sts[t // 2]["nsc"][:, t % 2 : t % 2 + 1],
-            )
+            c_ = sts[t // 2]["c"][:, t % 2 : t % 2 + 1]
+            nsc_ = sts[t // 2]["nsc"][:, t % 2 : t % 2 + 1]
+            if on_tensor(t):
+                for hf in range(2):
+                    nc.scalar.activation(
+                        out=ot[:, hf * 512 : (hf + 1) * 512], in_=pss[("j", t, hf)][:], func=ACT.Sigmoid, bias=c_, scale=nsc_
+                    )
+            else:
+                nc.scalar.activation(out=ot[:], in_=abs_[t][:, 1, :], func=ACT.Sigmoid, bias=c_, scale=nsc_)
             nc.sync.dma_start(out=out.rearrange("(p t) j -> p t j", t=NT)[:, t, :], in_=ot[:])
 
         w_transpose(0, 0, True)
@@ -322,7 +346,12 @@ def tile_layernormgrucell_pa_t_kernel(tc, x, h, W_irz, b_irz, W_hrz, b_hrz, out)
                 s_tr(it + 5)
             if it % 2 == 0 and ok(it - 2):
                 s_ch((it - 2) // 2)
-            if ok(it - LAG):
+                for t in (it - 2, it - 1):
+                    if on_tensor(t):
+                        s_diag(t)
+            if ok(it - LAG + 1) and on_tensor(it - LAG + 1):
+                s_join_pe(it - LAG + 1)
+            if ok(it - LAG) and not on_tensor(it - LAG):
                 s_p5(it - LAG)
             if ok(it):
                 if it >= HEAD:

from contextlib import ExitStack

import concourse.mybir as mybir
from concourse.masks import make_identity

F32 = mybir.dt.float32
BF16 = mybir.dt.bfloat16
U32 = mybir.dt.uint32
U8 = mybir.dt.uint8
FP8X4 = mybir.dt.float8_e4m3fn_x4
ALU = mybir.AluOpType
ACT = mybir.ActivationFunctionType

P = 128
B = 4096
K = 512
N = 1024
NT = B // P
EPS = 1e-5
FLOPS = 2 * 2 * B * K * N
CHUNKS = [(0, 2), (2, 2), (4, 4), (8, 8), (16, 8), (24, 8)]

LAG = 5
GP5 = 0
HEAD = 2
PEJ = 3
AB_BUFS = 8


def tile_layernormgrucell_pa_t_kernel(tc, x, h, W_irz, b_irz, W_hrz, b_hrz, out):
    nc = tc.nc
    with ExitStack() as ctx:
        const = ctx.enter_context(tc.tile_pool(name="const", bufs=1))
        wgp = ctx.enter_context(tc.tile_pool(name="wgp", bufs=2))
        xgp = ctx.enter_context(tc.tile_pool(name="xgp", bufs=3))
        xcp = ctx.enter_context(tc.tile_pool(name="xcp", bufs=3))
        abp = ctx.enter_context(tc.tile_pool(name="abp", bufs=AB_BUFS))
        op = ctx.enter_context(tc.tile_pool(name="op", bufs=4))
        jp = ctx.enter_context(tc.tile_pool(name="jp", bufs=2))
        stp = ctx.enter_context(tc.tile_pool(name="stp", bufs=AB_BUFS + 2))
        dgp = ctx.enter_context(tc.tile_pool(name="dgp", bufs=2))
        psp = ctx.enter_context(tc.psum_pool(name="psp", bufs=8))
        ctx.enter_context(tc.manual_schedule())

        def bank():
            return psp.tile([P, 512], F32, tag="bank", name="bank")

        ident = const.tile([P, P], F32, name="ident")
        make_identity(nc, ident[:])
        brow = const.tile([P, 2 * N], BF16, name="brow")
        nc.vector.memset(brow[:].bitcast(mybir.dt.int32), 0)
        ones = const.tile([P, P], BF16, name="ones")
        nc.vector.memset(ones[:], 1.0)
        mhalf = const.tile([P, 4], F32, name="mhalf")
        nc.vector.memset(mhalf[:], -0.5)
        warm = const.tile([P, 1], F32, name="warm")
        nc.scalar.activation(out=warm[:], in_=mhalf[:, 0:1], func=ACT.Sigmoid)

        acts = (x, h)
        wts = (W_irz, W_hrz)
        xch = [[None] * len(CHUNKS), [None] * len(CHUNKS)]
        wraw = [[None, None], [None, None]]

        def load_act(o, ci):
            t0, nt = CHUNKS[ci]
            t_ = const.tile([P, nt * K], BF16, name="act%d_%d" % (o, ci))
            nc.sync.dma_start(
                out=t_[:].rearrange("p (t k) -> p t k", k=K),
                in_=acts[o].rearrange("(p t) k -> p t k", t=NT)[:, t0 : t0 + nt, :],
            )
            xch[o][ci] = t_

        def load_w(o, hf):
            t_ = const.tile([P, 4 * K], BF16, name="wraw%d_%d" % (o, hf))
            nc.sync.dma_start(
                out=t_[:].rearrange("p (j k) -> p j k", k=K),
                in_=wts[o][hf * 512 : (hf + 1) * 512, :].rearrange("(j p) k -> p j k", p=P),
            )
            wraw[o][hf] = t_

        load_w(0, 0)
        load_act(0, 0)
        load_act(1, 0)
        nc.sync.dma_start(out=brow[0:1, 0:N], in_=b_irz.rearrange("(o n) -> o n", o=1))
        nc.sync.dma_start(out=brow[0:1, N : 2 * N], in_=b_hrz.rearrange("(o n) -> o n", o=1))
        load_w(0, 1)
        load_w(1, 0)
        load_w(1, 1)
        for ci in range(1, len(CHUNKS)):
            load_act(0, ci)
            load_act(1, ci)

        bias = const.tile([P, 2 * N], F32, name="bias")

        def spread_bias():
            for q in range(4):
                ps = bank()
                nc.tensor.matmul(out=ps[:], lhsT=ones[:], rhs=brow[:, q * 512 : (q + 1) * 512], start=True, stop=True)
                if q % 2 == 0:
                    nc.vector.tensor_copy(out=bias[:, q * 512 : (q + 1) * 512], in_=ps[:])
                else:
                    nc.scalar.copy(out=bias[:, q * 512 : (q + 1) * 512], in_=ps[:])

        wc = [const.tile([P, N], U32, name="wc%d" % o, align_bytes=64) for o in range(2)]
        wsc = [const.tile([P, N], U8, name="wsc%d" % o, align_bytes=64) for o in range(2)]
        wgs = {}

        def w_transpose(o, hf, second_on_vector):
            raw_w = wraw[o][hf][:].bitcast(F32)
            wg = wgp.tile([P, 2048], BF16, tag="wg", name="wg", align_bytes=64)
            wg_w = wg[:].bitcast(F32)
            for pr in range(2):
                tp = bank()
                for q in range(4):
                    c0 = pr * 512 + q * 128
                    nc.tensor.transpose(tp[:, q * P : (q + 1) * P], raw_w[:, c0 : c0 + 128], ident[:])
                dst = wg_w[:, pr * 512 : (pr + 1) * 512].rearrange("p (a r u) -> p a r u", a=2, u=2)
                src = tp[:].rearrange("p (a u r) -> p a r u", a=2, u=2)
                if pr == 1 and second_on_vector:
                    nc.vector.tensor_copy(out=dst, in_=src)
                else:
                    nc.scalar.copy(out=dst, in_=src)
            wgs[(o, hf)] = wg

        def w_quantise(o, hf):
            cols = slice(hf * 512, (hf + 1) * 512)
            nc.vector.quantize_mx(out=wc[o][:, cols].bitcast(FP8X4), scales=wsc[o][:, cols], in_=wgs[(o, hf)][:])

        def act_words(o, t):
            for ci in range(len(CHUNKS)):
                t0, nt = CHUNKS[ci]
                if t0 <= t < t0 + nt:
                    return xch[o][ci][:].bitcast(F32)[:, (t - t0) * 256 : (t - t0 + 1) * 256]
            raise ValueError("no chunk")

        dgs = {}
        tps = {}
        xgs = {}
        xcs = {}
        pss = {}
        abs_ = {}
        sts = {}

        def ok(t):
            return 0 <= t < NT

        def on_gpsimd(t):
            return GP5 > 0 and t % GP5 == GP5 - 1 and t < NT - 4

        def s_tr(t):
            tp = bank()
            for o in range(2):
                w_ = act_words(o, t)
                for u in range(2):
                    q = 2 * o + u
                    nc.tensor.transpose(tp[:, q * P : (q + 1) * P], w_[:, u * 128 : (u + 1) * 128], ident[:])
            tps[t] = tp

        def s_ev(t):
            xg = xgp.tile([P, 1024], BF16, tag="xg", name="xg", align_bytes=64)
            dst = xg[:].bitcast(F32).rearrange("p (a r u) -> p a r u", a=2, u=2)
            src = tps[t][:].rearrange("p (a u r) -> p a r u", a=2, u=2)
            if (t % 3 == 0) and t >= 4:
                nc.vector.tensor_copy(out=dst, in_=src)
            else:
                nc.scalar.copy(out=dst, in_=src)
            xgs[t] = xg

        def s_q(t):
            xc = xcp.tile([P, 256], U32, tag="xc", name="xc", align_bytes=64)
            xs = xcp.tile([P, 256], U8, tag="xs", name="xs", align_bytes=64)
            nc.vector.quantize_mx(out=xc[:].bitcast(FP8X4), scales=xs[:], in_=xgs[t][:])
            xcs[t] = (xc, xs)

        def s_mx(t, o, hf):
            xc, xs = xcs[t]
            cols = slice(hf * 512, (hf + 1) * 512)
            ps = bank()
            nc.tensor.matmul_mx(
                out=ps[:],
                lhsT=xc[:, o * P : (o + 1) * P].bitcast(FP8X4),
                lhsT_scale=xs[:, o * P : (o + 1) * P],
                rhs=wc[o][:, cols].bitcast(FP8X4),
                rhs_scale=wsc[o][:, cols],
                start=True,
                stop=True,
            )
            pss[(t, o, hf)] = ps

        def s_p1(t, o, hf):
            if (o, hf) == (0, 0):
                abs_[t] = abp.tile([P, 2, N], F32, tag="ab", name="ab")
                if t % 2 == 0:
                    sts[t // 2] = {
                        "sv": stp.tile([P, 2, 4], F32, tag="sv", name="sv"),
                        "ss": stp.tile([P, 4], F32, tag="ss", name="ss"),
                    }
            i = (t % 2) * 2 + o
            nc.vector.scalar_tensor_tensor(
                out=abs_[t][:, o, hf * 512 : (hf + 1) * 512],
                in0=pss[(t, o, hf)][:],
                scalar=-1.0,
                in1=bias[:, o * N + hf * 512 : o * N + (hf + 1) * 512],
                op0=ALU.mult,
                op1=ALU.subtract,
                accum_out=sts[t // 2]["sv"][:, hf, i : i + 1],
            )

        def s_sq(t, o):
            i = (t % 2) * 2 + o
            junk = jp.tile([P, N], BF16, tag="junk", name="junk")
            nc.scalar.activation(
                out=junk[:],
                in_=abs_[t][:, o, :],
                func=ACT.Square,
                bias=sts[t // 2]["sv"][:, 0, i : i + 1],
                scale=-512.0,
                accum_out=sts[t // 2]["ss"][:, i : i + 1],
            )

        def small(name, width):
            return stp.tile([P, width], F32, tag=name, name=name)

        def s_ch(m_):
            st = sts[m_]
            s0 = st["sv"][:, 0, :]
            s1 = st["sv"][:, 1, :]
            tt = nc.gpsimd.tensor_tensor
            dd = small("dd", 4)
            tt(out=dd[:], in0=s1, in1=s0, op=ALU.subtract)
            d2 = small("d2", 4)
            tt(out=d2[:], in0=dd[:], in1=dd[:], op=ALU.mult)
            sm = small("sm", 4)
            tt(out=sm[:], in0=s0, in1=s1, op=ALU.add)
            qq = small("qq", 4)
            nc.gpsimd.tensor_scalar(
                out=qq[:], in0=st["ss"][:], scalar1=1.0 / 256.0, scalar2=EPS * N * N, op0=ALU.mult, op1=ALU.add
            )
            vn = small("vn", 4)
            tt(out=vn[:], in0=qq[:], in1=d2[:], op=ALU.subtract)
            rsn = small("rsn", 4)
            tt(out=rsn[:], in0=vn[:], in1=mhalf[:], op=ALU.pow)
            vn_v = vn[:].rearrange("p (t o) -> p t o", o=2)
            rsn_v = rsn[:].rearrange("p (t o) -> p t o", o=2)
            sdn = small("sdn", 2)
            tt(out=sdn[:], in0=vn_v[:, :, 1], in1=rsn_v[:, :, 1], op=ALU.mult)
            rho = small("rho", 2)
            tt(out=rho[:], in0=sdn[:], in1=rsn_v[:, :, 0], op=ALU.mult)
            mm_ = small("mm_", 4)
            tt(out=mm_[:], in0=sm[:], in1=rsn[:], op=ALU.mult)
            mm_v = mm_[:].rearrange("p (t o) -> p t o", o=2)
            c = small("c", 2)
            tt(out=c[:], in0=mm_v[:, :, 0], in1=mm_v[:, :, 1], op=ALU.add)
            nsc = small("nsc", 2)
            nc.gpsimd.tensor_scalar(
                out=nsc[:], in0=rsn_v[:, :, 1], scalar1=-1.0 * N, scalar2=0.0, op0=ALU.mult, op1=ALU.add
            )
            st["rho"] = rho
            st["c"] = c
            st["nsc"] = nsc

        def on_tensor(t):
            return PEJ > 0 and t % PEJ == PEJ - 1

        def s_diag(t):
            dg = dgp.tile([P, P], F32, tag="dg", name="dg")
            nc.gpsimd.tensor_scalar(
                out=dg[:], in0=ident[:], scalar1=sts[t // 2]["rho"][:, t % 2 : t % 2 + 1], scalar2=0.0, op0=ALU.mult, op1=ALU.add
            )
            dgs[t] = dg

        def s_join_pe(t):
            ab = abs_[t]
            for hf in range(2):
                cols = slice(hf * 512, (hf + 1) * 512)
                ps = bank()
                nc.tensor.matmul(out=ps[:], lhsT=dgs[t][:], rhs=ab[:, 0, cols], start=True, stop=False)
                nc.tensor.matmul(out=ps[:], lhsT=ident[:], rhs=ab[:, 1, cols], start=False, stop=True)
                pss[("j", t, hf)] = ps

        def s_p5(t):
            ab = abs_[t]
            rho = sts[t // 2]["rho"][:, t % 2 : t % 2 + 1]
            if on_gpsimd(t):
                nc.gpsimd.tensor_scalar(out=ab[:, 0, :], in0=ab[:, 0, :], scalar1=rho, scalar2=0.0, op0=ALU.mult, op1=ALU.add)
                nc.gpsimd.tensor_tensor(out=ab[:, 1, :], in0=ab[:, 0, :], in1=ab[:, 1, :], op=ALU.add)
            else:
                nc.vector.scalar_tensor_tensor(
                    out=ab[:, 1, :], in0=ab[:, 0, :], scalar=rho, in1=ab[:, 1, :], op0=ALU.mult, op1=ALU.add
                )

        def s_sig(t):
            ot = op.tile([P, N], F32, tag="ot", name="ot")
            c_ = sts[t // 2]["c"][:, t % 2 : t % 2 + 1]
            nsc_ = sts[t // 2]["nsc"][:, t % 2 : t % 2 + 1]
            if on_tensor(t):
                for hf in range(2):
                    nc.scalar.activation(
                        out=ot[:, hf * 512 : (hf + 1) * 512], in_=pss[("j", t, hf)][:], func=ACT.Sigmoid, bias=c_, scale=nsc_
                    )
            else:
                nc.scalar.activation(out=ot[:], in_=abs_[t][:, 1, :], func=ACT.Sigmoid, bias=c_, scale=nsc_)
            nc.sync.dma_start(out=out.rearrange("(p t) j -> p t j", t=NT)[:, t, :], in_=ot[:])

        w_transpose(0, 0, True)
        w_quantise(0, 0)
        for t in range(HEAD):
            s_tr(t)
            s_ev(t)
            s_q(t)
        spread_bias()
        w_transpose(0, 1, False)
        for (o, hf) in ((0, 0), (0, 1), (1, 0), (1, 1)):
            for t in range(HEAD):
                s_mx(t, o, hf)
            for t in range(HEAD):
                s_p1(t, o, hf)
            if (o, hf) == (0, 0):
                w_quantise(0, 1)
                w_transpose(1, 0, False)
            if (o, hf) == (0, 1):
                w_quantise(1, 0)
                w_transpose(1, 1, False)
            if (o, hf) == (1, 0):
                w_quantise(1, 1)
                for t in range(HEAD):
                    s_sq(t, 0)
                for t in (2, 3):
                    s_tr(t)
                    s_ev(t)
        s_q(2)
        s_tr(4)

        for it in range(NT + LAG):
            if ok(it + 2) and it + 2 > HEAD:
                s_q(it + 2)
            if ok(it) and it >= HEAD:
                for o in range(2):
                    for hf in range(2):
                        s_p1(it, o, hf)
            if ok(it + 1) and it + 1 >= HEAD:
                for o in range(2):
                    for hf in range(2):
                        s_mx(it + 1, o, hf)
            if ok(it + 5):
                s_tr(it + 5)
            if it % 2 == 0 and ok(it - 2):
                s_ch((it - 2) // 2)
                for t in (it - 2, it - 1):
                    if on_tensor(t):
                        s_diag(t)
            if ok(it - LAG + 1) and on_tensor(it - LAG + 1):
                s_join_pe(it - LAG + 1)
            if ok(it - LAG) and not on_tensor(it - LAG):
                s_p5(it - LAG)
            if ok(it):
                if it >= HEAD:
                    s_sq(it, 0)
                s_sq(it, 1)
            if ok(it - LAG):
                s_sig(it - LAG)
            if ok(it + 4):
                s_ev(it + 4)
